import numpy as np
import ml_dtypes


BF16 = ml_dtypes.bfloat16


def bf(x):
    return np.asarray(x, np.float32).astype(BF16)


def f64(x):
    return np.asarray(x).astype(np.float64)


E2M1 = np.array([0.0, 0.5, 1.0, 1.5, 2.0, 3.0, 4.0, 6.0, -0.0, -0.5, -1.0, -1.5, -2.0, -3.0, -4.0, -6.0])


def pack_weight(w, fmt):
    k, n = w.shape
    w = f64(bf(w)).reshape(k // 32, 32, n)
    amax = np.abs(w).max(1)
    if fmt == "e4m3":
        byte = np.frexp(amax)[1] - 1 + 127 - 7
    else:
        mant, ex = np.frexp(amax / 6.0)
        byte = np.where(mant > 0.5, ex, ex - 1) + 127
    byte = np.clip(np.where(amax > 0, byte, 1), 1, 254)
    scaled = (w * np.exp2(127.0 - byte)[:, None, :]).reshape(k, n).astype(np.float32)
    by_word = np.ascontiguousarray(scaled.reshape(k // 512, 128, 4, n).transpose(0, 1, 3, 2))
    if fmt == "e4m3":
        words = by_word.astype(ml_dtypes.float8_e4m3fn).view(np.uint8)
    else:
        c = by_word.astype(ml_dtypes.float4_e2m1fn).view(np.uint8) & 0xF
        words = c[..., 0::2] | (c[..., 1::2] << 4)
    return np.ascontiguousarray(words), np.ascontiguousarray(byte.astype(np.uint8).reshape(k // 512, 16, n))


def unpack_weight(words, scales, fmt):
    g, p, n, _ = words.shape
    if fmt == "e4m3":
        vals = np.ascontiguousarray(words).view(ml_dtypes.float8_e4m3fn).astype(np.float64)
    else:
        nib = np.empty((g, p, n, 4), np.uint8)
        nib[..., 0::2] = words & 0xF
        nib[..., 1::2] = words >> 4
        vals = E2M1[nib]
    vals = vals * np.repeat(np.exp2(scales.astype(np.float64) - 127.0), 8, axis=1)[..., None]
    return vals.transpose(0, 1, 3, 2).reshape(g * 512, n)

def pack4(w):
    words, scales = pack_weight(w, "e2m1")
    return words.reshape(words.shape[0], 128, -1), scales


def unpack4(words, scales):
    return unpack_weight(words.reshape(words.shape[0], 128, -1, 2), scales, "e2m1")


def kspread(k):
    return np.exp2(np.repeat(np.random.randint(-6, 7, k // 32), 32).astype(np.float64))


B, N, D, H, DH = 2, 256, 2048, 8, 128
E = H * DH
HALF = DH // 2
EPS = 1e-6
ROPE_BASE = 10000.0
GAIN = np.sqrt(1.8 / DH)


def rmsnorm(t):
    return t * (1.0 / np.sqrt(np.mean(t * t, axis=-1, keepdims=True) + EPS))


def rope(t):
    inv_freq = 1.0 / (ROPE_BASE ** (np.arange(0, DH, 2, dtype=np.float64) / DH))
    ang = np.arange(N, dtype=np.float64)[:, None] * inv_freq[None, :]
    cos, sin = np.cos(ang), np.sin(ang)
    t1, t2 = t[..., :HALF], t[..., HALF:]
    return np.concatenate([t1 * cos - t2 * sin, t1 * sin + t2 * cos], axis=-1)


def heads(t):
    return t.reshape(B, N, H, DH).transpose(0, 2, 1, 3)


def setup_inputs():
    s = kspread(D)
    x = np.random.standard_normal((B, N, D)) * s
    x_words, x_scales = pack4(np.ascontiguousarray(x.reshape(B * N, D).T))
    words, scales = pack4(np.random.standard_normal((D, 3 * E)) * D ** -0.5 / s[:, None])
    scale_param = bf(GAIN * (1.0 + 0.1 * np.random.standard_normal((H, DH))) * D ** -0.5)
    return {"x_words": x_words,
            "x_scales": x_scales,
            "w_qkv_words": words,
            "w_qkv_scales": scales,
            "scale_param": scale_param}


def reference(x_words, x_scales, w_qkv_words, w_qkv_scales, scale_param):
    qkv = unpack4(x_words, x_scales).T.reshape(B, N, D) @ unpack4(w_qkv_words, w_qkv_scales)
    q, k, v = np.split(qkv, 3, axis=-1)
    q, k, v = heads(q), heads(k), heads(v)
    scaler = (f64(scale_param) * (1.0 / (D ** -0.5)))[None, :, None, :]
    q = rmsnorm(q) * scaler
    k = rmsnorm(k) * scaler
    return rope(q), rope(k), v

@@ -1,0 +1,234 @@
+from contextlib import ExitStack
+
+import concourse.mybir as mybir
+
+F32 = mybir.dt.float32
+BF16 = mybir.dt.bfloat16
+U8 = mybir.dt.uint8
+I32 = mybir.dt.int32
+FP4 = mybir.dt.float4_e2m1fn_x4
+ALU = mybir.AluOpType
+ACT = mybir.ActivationFunctionType
+
+P = 128
+PASSES = 4
+TOKENS = 512
+D_IN = 2048
+E = 1024
+DH = 128
+HALF = 64
+EPS = 1e-6
+TWO_PI = 6.283185307179586
+RATIO = 10000.0 ** (-1.0 / 64.0)
+
+FLOPS = 2 * TOKENS * D_IN * 3 * E
+
+Q, K, V = 0, 1, 2
+M_ORDER = (0, 2, 1, 3)
+
+
+def tile_attn_pa_kernel(tc, x_words, x_scales, w_words, w_scales, scale_param, out_q, out_k, out_v):
+    nc = tc.nc
+    outs = (out_q, out_k, out_v)
+
+    with ExitStack() as ctx:
+        const = ctx.enter_context(tc.tile_pool(name="const", bufs=1))
+        work = ctx.enter_context(tc.tile_pool(name="work", bufs=4))
+        psum = ctx.enter_context(tc.psum_pool(name="psum", bufs=8))
+        ctx.enter_context(tc.manual_schedule())
+
+        xw = []
+        wq = []
+        for g in range(PASSES):
+            xw_g = const.tile([P, 2 * TOKENS], U8, name="xw%d" % g, align_bytes=64)
+            xw.append(xw_g)
+            wq_g = const.tile([P, 2 * E], U8, name="wq%d" % g, align_bytes=64)
+            wq.append(wq_g)
+        xs = const.tile([P, PASSES, TOKENS], U8, name="xs", align_bytes=64)
+        wk = const.tile([P, PASSES, 2 * E], U8, name="wk", align_bytes=64)
+        wv = const.tile([P, PASSES, 2 * E], U8, name="wv", align_bytes=64)
+        ws = []
+        for pr in range(3):
+            ws_pr = const.tile([P, PASSES, E], U8, name="ws%d" % pr, align_bytes=64)
+            ws.append(ws_pr)
+        g_row = const.tile([P, E], BF16, name="g_row")
+        ones = const.tile([P, P], BF16, name="ones")
+        warm = const.tile([P, 1], F32, name="warm")
+        pos = const.tile([P, 2], F32, name="pos")
+        pos_turns = const.tile([P, 2], F32, name="pos_turns")
+        freq = const.tile([P, HALF], F32, name="freq")
+        turns = const.tile([P, 2, 2, HALF], F32, name="turns")
+        whole = const.tile([P, 4 * HALF], I32, name="whole")
+        frac = const.tile([P, 4 * HALF], F32, name="frac")
+        negf = const.tile([P, 2, 2, HALF], F32, name="negf")
+        trig = const.tile([P, 2, 3, HALF], F32, name="trig")
+        tab_a = {}
+        tab_b = {}
+        for t in range(2):
+            for cb in range(2):
+                tab_a[(t, cb)] = const.tile([P, 512], F32, name="tab_a%d%d" % (t, cb))
+                tab_b[(t, cb)] = const.tile([P, 512], F32, name="tab_b%d%d" % (t, cb))
+
+        def w_codes(pr, g, cb):
+            cols = slice(1024 * cb, 1024 * (cb + 1))
+            if pr == Q:
+                return wq[g][:, cols]
+            if pr == K:
+                return wk[:, g, cols]
+            return wv[:, g, cols]
+
+        def load_scales(plane, src):
+            for quad in range(4):
+                nc.sync.dma_start(
+                    out=plane[32 * quad : 32 * quad + 4, :, :].bitcast(I32),
+                    in_=src[:, 4 * quad : 4 * quad + 4, :].rearrange("g r n -> r g n").bitcast(I32),
+                )
+
+        def load_x(g):
+            nc.sync.dma_start(out=xw[g][:].bitcast(I32), in_=x_words[g].bitcast(I32))
+
+        def load_wq(g):
+            nc.sync.dma_start(out=wq[g][:].bitcast(I32), in_=w_words[g][:, 0 : 2 * E].bitcast(I32))
+
+        nc.gpsimd.memset(warm[:], 0.0)
+        nc.scalar.activation(out=warm[:], in_=warm[:], func=ACT.Sin)
+        nc.vector.memset(xs[:].bitcast(I32), 0)
+        nc.vector.memset(ws[Q][:].bitcast(I32), 0)
+        nc.vector.memset(g_row[:], 0.0)
+        nc.vector.memset(ones[:], 1.0)
+        load_x(0)
+        load_wq(0)
+        load_scales(xs, x_scales)
+        load_scales(ws[Q], w_scales[:, :, 0:E])
+        nc.scalar.dma_start(out=g_row[0:1, :], in_=scale_param.rearrange("h d -> (h d)").unsqueeze(0))
+        for g in range(1, PASSES):
+            load_x(g)
+            load_wq(g)
+        nc.vector.memset(ws[V][:].bitcast(I32), 0)
+        nc.vector.memset(ws[K][:].bitcast(I32), 0)
+        load_scales(ws[V], w_scales[:, :, 2 * E : 3 * E])
+        nc.sync.dma_start(out=wv[:].bitcast(I32), in_=w_words[:, :, 4 * E : 6 * E].rearrange("g p n -> p g n").bitcast(I32))
+        load_scales(ws[K], w_scales[:, :, E : 2 * E])
+        nc.sync.dma_start(out=wk[:].bitcast(I32), in_=w_words[:, :, 2 * E : 4 * E].rearrange("g p n -> p g n").bitcast(I32))
+
+        nc.gpsimd.iota(pos[:], pattern=[[P, 2]], base=0, channel_multiplier=1, allow_small_or_imprecise_dtypes=True)
+        nc.gpsimd.memset(freq[:, 0:1], 1.0)
+        for w in (1, 2, 4, 8, 16, 32):
+            nc.gpsimd.tensor_scalar(
+                out=freq[:, w : 2 * w], in0=freq[:, 0:w], scalar1=RATIO**w, scalar2=0.0, op0=ALU.mult, op1=ALU.add
+            )
+        nc.vector.tensor_scalar(out=pos_turns[:], in0=pos[:], scalar1=1.0 / TWO_PI, scalar2=None, op0=ALU.mult)
+        for t in range(2):
+            for s, off in enumerate((0.25, 0.0)):
+                nc.vector.tensor_scalar(
+                    out=turns[:, t, s, :], in0=freq[:], scalar1=pos_turns[:, t : t + 1], scalar2=off, op0=ALU.mult, op1=ALU.add
+                )
+        turns_flat = turns[:].rearrange("p t s j -> p (t s j)")
+        nc.vector.tensor_copy(out=whole[:], in_=turns_flat)
+        nc.vector.tensor_tensor(out=frac[:], in0=turns_flat, in1=whole[:], op=ALU.subtract)
+        nc.vector.scalar_tensor_tensor(
+            out=negf[:].rearrange("p t s j -> p (t s j)"), in0=frac[:], scalar=0.5, in1=frac[:], op0=ALU.is_gt, op1=ALU.subtract
+        )
+        nc.scalar.activation(out=trig[:, :, 0:2, :], in_=negf[:], func=ACT.Sin, scale=-TWO_PI)
+        nc.scalar.activation(out=warm[:], in_=warm[:], func=ACT.Abs_reciprocal_sqrt, bias=1.0)
+        nc.vector.tensor_scalar(out=trig[:, :, 2, :], in0=trig[:, :, 1, :], scalar1=-1.0, scalar2=None, op0=ALU.mult)
+
+        def build_tables(t, cb, gain):
+            nc.vector.tensor_tensor(
+                out=tab_a[(t, cb)][:].rearrange("p (a j) -> p a j", j=HALF),
+                in0=gain.rearrange("p (a j) -> p a j", j=HALF),
+                in1=trig[:, t, 0, :].unsqueeze(1).to_broadcast([P, 8, HALF]),
+                op=ALU.mult,
+            )
+            nc.vector.tensor_tensor(
+                out=tab_b[(t, cb)][:].rearrange("p (h d) -> p h d", d=DH),
+                in0=gain.rearrange("p (h d) -> p h d", d=DH),
+                in1=trig[:, t, 1:3, :].rearrange("p s j -> p (s j)").unsqueeze(1).to_broadcast([P, 4, DH]),
+                op=ALU.mult,
+            )
+
+        def mx_pass(acc, pr, cb, m, g):
+            nc.tensor.matmul_mx(
+                out=acc[:],
+                lhsT=xw[g][:, 256 * m : 256 * (m + 1)].bitcast(FP4),
+                lhsT_scale=xs[:, g, P * m : P * (m + 1)],
+                rhs=w_codes(pr, g, cb).bitcast(FP4),
+                rhs_scale=ws[pr][:, g, 512 * cb : 512 * (cb + 1)],
+                start=(g == 0),
+                stop=(g == PASSES - 1),
+            )
+
+        def dest(pr, cb, m):
+            b, t = m // 2, m % 2
+            return outs[pr][b, 4 * cb : 4 * cb + 4, P * t : P * (t + 1), :].rearrange("h p d -> p h d")
+
+        def qk_epilogue(acc, pr, cb, m):
+            t = m % 2
+            ss = work.tile([P, 4], F32, tag="ss", bufs=4, name="ss")
+            for h in range(4):
+                junk = work.tile([P, DH], F32, tag="junk", bufs=2, name="junk")
+                nc.scalar.activation(
+                    out=junk[:], in_=acc[:, DH * h : DH * (h + 1)], func=ACT.Square, accum_out=ss[:, h : h + 1]
+                )
+            rinv = work.tile([P, 4], F32, tag="rinv", bufs=4, name="rinv")
+            nc.scalar.activation(
+                out=rinv[:], in_=ss[:], func=ACT.Abs_reciprocal_sqrt, scale=1.0 / (DH * D_IN), bias=EPS / D_IN
+            )
+            t1 = work.tile([P, 512], F32, tag="t1", bufs=6, name="t1")
+            t2 = work.tile([P, 512], F32, tag="t2", bufs=4, name="t2")
+            for h in range(4):
+                hs = slice(DH * h, DH * (h + 1))
+                nc.vector.scalar_tensor_tensor(
+                    out=t1[:, hs], in0=acc[:, hs], scalar=rinv[:, h : h + 1], in1=tab_a[(t, cb)][:, hs], op0=ALU.mult, op1=ALU.mult
+                )
+                nc.vector.scalar_tensor_tensor(
+                    out=t2[:, hs], in0=acc[:, hs], scalar=rinv[:, h : h + 1], in1=tab_b[(t, cb)][:, hs], op0=ALU.mult, op1=ALU.mult
+                )
+            nc.gpsimd.tensor_tensor(
+                out=t1[:].rearrange("p (h s j) -> p h s j", s=2, j=HALF),
+                in0=t1[:].rearrange("p (h s j) -> p h s j", s=2, j=HALF),
+                in1=t2[:].rearrange("p (h s j) -> p h s j", s=2, j=HALF)[:, :, ::-1, :],
+                op=ALU.add,
+            )
+            nc.sync.dma_start(out=dest(pr, cb, m), in_=t1[:].rearrange("p (h d) -> p h d", d=DH))
+
+        def v_epilogue(acc, cb, m):
+            vo = work.tile([P, 512], F32, tag="vo", bufs=4, name="vo")
+            nc.scalar.copy(out=vo[:], in_=acc[:])
+            nc.scalar.dma_start(out=dest(V, cb, m), in_=vo[:].rearrange("p (h d) -> p h d", d=DH))
+
+        first = []
+        for m in M_ORDER:
+            acc0 = psum.tile([P, 512], F32, tag="acc", name="acc0")
+            first.append(acc0)
+        for g in range(PASSES):
+            for i, m in enumerate(M_ORDER):
+                mx_pass(first[i], Q, 0, m, g)
+            if g == 0:
+                g_ps = []
+                for cb in range(2):
+                    g_half = psum.tile([P, 512], F32, tag="acc", name="g_half%d" % cb)
+                    nc.tensor.matmul(out=g_half[:], lhsT=ones[:], rhs=g_row[:, 512 * cb : 512 * (cb + 1)], start=True, stop=True)
+                    g_ps.append(g_half)
+                for cb in range(2):
+                    for t in range(2):
+                        build_tables(t, cb, g_ps[cb][:])
+        for i, m in enumerate(M_ORDER):
+            qk_epilogue(first[i], Q, 0, m)
+
+        heavy = [(pr, cb, m) for pr, cb in ((Q, 1), (K, 0), (K, 1)) for m in M_ORDER]
+        light = [(V, cb, m) for cb in range(2) for m in M_ORDER]
+        rest = []
+        for i in range(6):
+            rest.extend([heavy[2 * i], heavy[2 * i + 1]])
+            if i < 5:
+                rest.append(light[i])
+        rest.extend(light[5:])
+        for pr, cb, m in rest:
+            acc = psum.tile([P, 512], F32, tag="acc", name="acc")
+            for g in range(PASSES):
+                mx_pass(acc, pr, cb, m, g)
+            if pr == V:
+                v_epilogue(acc, cb, m)
+            else:
+                qk_epilogue(acc, pr, cb, m)

@@ -25,6 +25,8 @@ FLOPS = 2 * TOKENS * D_IN * 3 * E
 
 Q, K, V = 0, 1, 2
 M_ORDER = (0, 2, 1, 3)
+N_IDLE = 10
+ADD_SIZES = (1, 1, 2, 2, 2, 2, 2, 2, 1, 1)
 
 
 def tile_attn_pa_kernel(tc, x_words, x_scales, w_words, w_scales, scale_param, out_q, out_k, out_v):
@@ -53,6 +55,7 @@ def tile_attn_pa_kernel(tc, x_words, x_scales, w_words, w_scales, scale_param, o
             ws.append(ws_pr)
         g_row = const.tile([P, E], BF16, name="g_row")
         ones = const.tile([P, P], BF16, name="ones")
+        idle_rhs = const.tile([P, 512], BF16, name="idle_rhs")
         warm = const.tile([P, 1], F32, name="warm")
         pos = const.tile([P, 2], F32, name="pos")
         pos_turns = const.tile([P, 2], F32, name="pos_turns")
@@ -90,31 +93,27 @@ def tile_attn_pa_kernel(tc, x_words, x_scales, w_words, w_scales, scale_param, o
         def load_wq(g):
             nc.sync.dma_start(out=wq[g][:].bitcast(I32), in_=w_words[g][:, 0 : 2 * E].bitcast(I32))
 
+        load_x(0)
+        load_wq(0)
         nc.gpsimd.memset(warm[:], 0.0)
+        nc.vector.memset(ones[:], 1.0)
+        nc.vector.memset(idle_rhs[:], 0.0)
+        nc.vector.memset(g_row[:], 0.0)
+        nc.scalar.dma_start(out=g_row[0:1, :], in_=scale_param.rearrange("h d -> (h d)").unsqueeze(0))
         nc.scalar.activation(out=warm[:], in_=warm[:], func=ACT.Sin)
         nc.vector.memset(xs[:].bitcast(I32), 0)
         nc.vector.memset(ws[Q][:].bitcast(I32), 0)
-        nc.vector.memset(g_row[:], 0.0)
-        nc.vector.memset(ones[:], 1.0)
-        load_x(0)
-        load_wq(0)
         load_scales(xs, x_scales)
         load_scales(ws[Q], w_scales[:, :, 0:E])
-        nc.scalar.dma_start(out=g_row[0:1, :], in_=scale_param.rearrange("h d -> (h d)").unsqueeze(0))
         for g in range(1, PASSES):
             load_x(g)
             load_wq(g)
-        nc.vector.memset(ws[V][:].bitcast(I32), 0)
-        nc.vector.memset(ws[K][:].bitcast(I32), 0)
-        load_scales(ws[V], w_scales[:, :, 2 * E : 3 * E])
-        nc.sync.dma_start(out=wv[:].bitcast(I32), in_=w_words[:, :, 4 * E : 6 * E].rearrange("g p n -> p g n").bitcast(I32))
-        load_scales(ws[K], w_scales[:, :, E : 2 * E])
-        nc.sync.dma_start(out=wk[:].bitcast(I32), in_=w_words[:, :, 2 * E : 4 * E].rearrange("g p n -> p g n").bitcast(I32))
 
         nc.gpsimd.iota(pos[:], pattern=[[P, 2]], base=0, channel_multiplier=1, allow_small_or_imprecise_dtypes=True)
-        nc.gpsimd.memset(freq[:, 0:1], 1.0)
+        chain = nc.gpsimd
+        chain.memset(freq[:, 0:1], 1.0)
         for w in (1, 2, 4, 8, 16, 32):
-            nc.gpsimd.tensor_scalar(
+            chain.tensor_scalar(
                 out=freq[:, w : 2 * w], in0=freq[:, 0:w], scalar1=RATIO**w, scalar2=0.0, op0=ALU.mult, op1=ALU.add
             )
         nc.vector.tensor_scalar(out=pos_turns[:], in0=pos[:], scalar1=1.0 / TWO_PI, scalar2=None, op0=ALU.mult)
@@ -131,6 +130,14 @@ def tile_attn_pa_kernel(tc, x_words, x_scales, w_words, w_scales, scale_param, o
         )
         nc.scalar.activation(out=trig[:, :, 0:2, :], in_=negf[:], func=ACT.Sin, scale=-TWO_PI)
         nc.scalar.activation(out=warm[:], in_=warm[:], func=ACT.Abs_reciprocal_sqrt, bias=1.0)
+
+        nc.vector.memset(ws[V][:].bitcast(I32), 0)
+        nc.vector.memset(ws[K][:].bitcast(I32), 0)
+        load_scales(ws[V], w_scales[:, :, 2 * E : 3 * E])
+        nc.sync.dma_start(out=wv[:].bitcast(I32), in_=w_words[:, :, 4 * E : 6 * E].rearrange("g p n -> p g n").bitcast(I32))
+        load_scales(ws[K], w_scales[:, :, E : 2 * E])
+        nc.sync.dma_start(out=wk[:].bitcast(I32), in_=w_words[:, :, 2 * E : 4 * E].rearrange("g p n -> p g n").bitcast(I32))
+
         nc.vector.tensor_scalar(out=trig[:, :, 2, :], in0=trig[:, :, 1, :], scalar1=-1.0, scalar2=None, op0=ALU.mult)
 
         def build_tables(t, cb, gain):
@@ -162,6 +169,9 @@ def tile_attn_pa_kernel(tc, x_words, x_scales, w_words, w_scales, scale_param, o
             b, t = m // 2, m % 2
             return outs[pr][b, 4 * cb : 4 * cb + 4, P * t : P * (t + 1), :].rearrange("h p d -> p h d")
 
+        pair = []
+        sizes = list(ADD_SIZES)
+
         def qk_epilogue(acc, pr, cb, m):
             t = m % 2
             ss = work.tile([P, 4], F32, tag="ss", bufs=4, name="ss")
@@ -174,28 +184,54 @@ def tile_attn_pa_kernel(tc, x_words, x_scales, w_words, w_scales, scale_param, o
             nc.scalar.activation(
                 out=rinv[:], in_=ss[:], func=ACT.Abs_reciprocal_sqrt, scale=1.0 / (DH * D_IN), bias=EPS / D_IN
             )
-            t1 = work.tile([P, 512], F32, tag="t1", bufs=6, name="t1")
-            t2 = work.tile([P, 512], F32, tag="t2", bufs=4, name="t2")
+            if not pair:
+                t1_new = work.tile([P, 2 * 512], F32, tag="t1", bufs=4, name="t1")
+                t2_new = work.tile([P, 2 * 512], F32, tag="t2", bufs=3, name="t2")
+                pair.append((t1_new, t2_new))
+            t1, t2 = pair[0]
+            base = 512 * (len(pair) - 1)
+            pair.append((pr, cb, m))
             for h in range(4):
                 hs = slice(DH * h, DH * (h + 1))
+                t_cols = slice(base + DH * h, base + DH * (h + 1))
                 nc.vector.scalar_tensor_tensor(
-                    out=t1[:, hs], in0=acc[:, hs], scalar=rinv[:, h : h + 1], in1=tab_a[(t, cb)][:, hs], op0=ALU.mult, op1=ALU.mult
+                    out=t1[:, t_cols], in0=acc[:, hs], scalar=rinv[:, h : h + 1], in1=tab_a[(t, cb)][:, hs], op0=ALU.mult, op1=ALU.mult
                 )
                 nc.vector.scalar_tensor_tensor(
-                    out=t2[:, hs], in0=acc[:, hs], scalar=rinv[:, h : h + 1], in1=tab_b[(t, cb)][:, hs], op0=ALU.mult, op1=ALU.mult
+                    out=t2[:, t_cols], in0=acc[:, hs], scalar=rinv[:, h : h + 1], in1=tab_b[(t, cb)][:, hs], op0=ALU.mult, op1=ALU.mult
                 )
-            nc.gpsimd.tensor_tensor(
-                out=t1[:].rearrange("p (h s j) -> p h s j", s=2, j=HALF),
-                in0=t1[:].rearrange("p (h s j) -> p h s j", s=2, j=HALF),
-                in1=t2[:].rearrange("p (h s j) -> p h s j", s=2, j=HALF)[:, :, ::-1, :],
-                op=ALU.add,
-            )
-            nc.sync.dma_start(out=dest(pr, cb, m), in_=t1[:].rearrange("p (h d) -> p h d", d=DH))
+            if len(pair) == sizes[0] + 1:
+                width = 512 * sizes[0]
+                sizes.remove(sizes[0])
+                nc.gpsimd.tensor_tensor(
+                    out=t1[:, 0:width].rearrange("p (a s j) -> p a s j", s=2, j=HALF),
+                    in0=t1[:, 0:width].rearrange("p (a s j) -> p a s j", s=2, j=HALF),
+                    in1=t2[:, 0:width].rearrange("p (a s j) -> p a s j", s=2, j=HALF)[:, :, ::-1, :],
+                    op=ALU.add,
+                )
+                for i, group in enumerate(pair[1:]):
+                    nc.sync.dma_start(
+                        out=dest(group[0], group[1], group[2]),
+                        in_=t1[:, 512 * i : 512 * (i + 1)].rearrange("p (h d) -> p h d", d=DH),
+                    )
+                pair.clear()
 
         def v_epilogue(acc, cb, m):
             vo = work.tile([P, 512], F32, tag="vo", bufs=4, name="vo")
             nc.scalar.copy(out=vo[:], in_=acc[:])
             nc.scalar.dma_start(out=dest(V, cb, m), in_=vo[:].rearrange("p (h d) -> p h d", d=DH))
+
+        idle_ps = psum.tile([P, 512], F32, tag="acc", name="idle_ps")
+        for i in range(N_IDLE):
+            nc.tensor.matmul(out=idle_ps[:], lhsT=ones[:], rhs=idle_rhs[:], start=True, stop=True)
+        g_ps = []
+        for cb in range(2):
+            g_half = psum.tile([P, 512], F32, tag="acc", name="g_half%d" % cb)
+            nc.tensor.matmul(out=g_half[:], lhsT=ones[:], rhs=g_row[:, 512 * cb : 512 * (cb + 1)], start=True, stop=True)
+            g_ps.append(g_half)
+        for cb in range(2):
+            for t in range(2):
+                build_tables(t, cb, g_ps[cb][:])
 
         first = []
         for m in M_ORDER:
@@ -204,15 +240,6 @@ def tile_attn_pa_kernel(tc, x_words, x_scales, w_words, w_scales, scale_param, o
         for g in range(PASSES):
             for i, m in enumerate(M_ORDER):
                 mx_pass(first[i], Q, 0, m, g)
-            if g == 0:
-                g_ps = []
-                for cb in range(2):
-                    g_half = psum.tile([P, 512], F32, tag="acc", name="g_half%d" % cb)
-                    nc.tensor.matmul(out=g_half[:], lhsT=ones[:], rhs=g_row[:, 512 * cb : 512 * (cb + 1)], start=True, stop=True)
-                    g_ps.append(g_half)
-                for cb in range(2):
-                    for t in range(2):
-                        build_tables(t, cb, g_ps[cb][:])
         for i, m in enumerate(M_ORDER):
             qk_epilogue(first[i], Q, 0, m)
 
@@ -221,9 +248,9 @@ def tile_attn_pa_kernel(tc, x_words, x_scales, w_words, w_scales, scale_param, o
         rest = []
         for i in range(6):
             rest.extend([heavy[2 * i], heavy[2 * i + 1]])
-            if i < 5:
+            if i < 4:
                 rest.append(light[i])
-        rest.extend(light[5:])
+        rest.extend(light[4:7])
         for pr, cb, m in rest:
             acc = psum.tile([P, 512], F32, tag="acc", name="acc")
             for g in range(PASSES):
@@ -232,3 +259,26 @@ def tile_attn_pa_kernel(tc, x_words, x_scales, w_words, w_scales, scale_param, o
                 v_epilogue(acc, cb, m)
             else:
                 qk_epilogue(acc, pr, cb, m)
+
+        pr, cb, m = light[7]
+        for half in range(2):
+            acc_h = psum.tile([P, 512], F32, tag="acc", name="acc_h")
+            for g in range(PASSES):
+                nc.tensor.matmul_mx(
+                    out=acc_h[:, 0:256],
+                    lhsT=xw[g][:, 256 * m : 256 * (m + 1)].bitcast(FP4),
+                    lhsT_scale=xs[:, g, P * m : P * (m + 1)],
+                    rhs=wv[:, g, 1024 * cb + 512 * half : 1024 * cb + 512 * (half + 1)].bitcast(FP4),
+                    rhs_scale=ws[V][:, g, 512 * cb + 256 * half : 512 * cb + 256 * (half + 1)],
+                    start=(g == 0),
+                    stop=(g == PASSES - 1),
+                )
+            vh = work.tile([P, 256], F32, tag="vh", bufs=2, name="vh")
+            b, t = m // 2, m % 2
+            dst = out_v[b, 4 * cb + 2 * half : 4 * cb + 2 * half + 2, P * t : P * (t + 1), :].rearrange("h p d -> p h d")
+            if half == 0:
+                nc.scalar.copy(out=vh[:], in_=acc_h[:, 0:256])
+                nc.scalar.dma_start(out=dst, in_=vh[:].rearrange("p (h d) -> p h d", d=DH))
+            else:
+                nc.vector.tensor_copy(out=vh[:], in_=acc_h[:, 0:256])
+                nc.sync.dma_start(out=dst, in_=vh[:].rearrange("p (h d) -> p h d", d=DH))

@@ -25,7 +25,7 @@ FLOPS = 2 * TOKENS * D_IN * 3 * E
 
 Q, K, V = 0, 1, 2
 M_ORDER = (0, 2, 1, 3)
-N_IDLE = 10
+N_IDLE = 12
 ADD_SIZES = (1, 1, 2, 2, 2, 2, 2, 2, 1, 1)
 
 
@@ -53,6 +53,10 @@ def tile_attn_pa_kernel(tc, x_words, x_scales, w_words, w_scales, scale_param, o
         for pr in range(3):
             ws_pr = const.tile([P, PASSES, E], U8, name="ws%d" % pr, align_bytes=64)
             ws.append(ws_pr)
+        wsq = []
+        for cb in range(2):
+            wsq_cb = const.tile([P, PASSES, 512], U8, name="wsq%d" % cb, align_bytes=64)
+            wsq.append(wsq_cb)
         g_row = const.tile([P, E], BF16, name="g_row")
         ones = const.tile([P, P], BF16, name="ones")
         idle_rhs = const.tile([P, 512], BF16, name="idle_rhs")
@@ -93,21 +97,23 @@ def tile_attn_pa_kernel(tc, x_words, x_scales, w_words, w_scales, scale_param, o
         def load_wq(g):
             nc.sync.dma_start(out=wq[g][:].bitcast(I32), in_=w_words[g][:, 0 : 2 * E].bitcast(I32))
 
-        load_x(0)
-        load_wq(0)
         nc.gpsimd.memset(warm[:], 0.0)
+        nc.scalar.activation(out=warm[:], in_=warm[:], func=ACT.Sin)
+        nc.vector.memset(xs[:].bitcast(I32), 0)
+        nc.vector.memset(wsq[0][:].bitcast(I32), 0)
+        load_scales(xs, x_scales)
+        load_scales(wsq[0], w_scales[:, :, 0:512])
         nc.vector.memset(ones[:], 1.0)
         nc.vector.memset(idle_rhs[:], 0.0)
         nc.vector.memset(g_row[:], 0.0)
-        nc.scalar.dma_start(out=g_row[0:1, :], in_=scale_param.rearrange("h d -> (h d)").unsqueeze(0))
-        nc.scalar.activation(out=warm[:], in_=warm[:], func=ACT.Sin)
-        nc.vector.memset(xs[:].bitcast(I32), 0)
-        nc.vector.memset(ws[Q][:].bitcast(I32), 0)
-        load_scales(xs, x_scales)
-        load_scales(ws[Q], w_scales[:, :, 0:E])
+        nc.vector.memset(wsq[1][:].bitcast(I32), 0)
+        load_x(0)
+        load_wq(0)
+        nc.sync.dma_start(out=g_row[0:1, :], in_=scale_param.rearrange("h d -> (h d)").unsqueeze(0))
         for g in range(1, PASSES):
             load_x(g)
             load_wq(g)
+        load_scales(wsq[1], w_scales[:, :, 512:E])
 
         nc.gpsimd.iota(pos[:], pattern=[[P, 2]], base=0, channel_multiplier=1, allow_small_or_imprecise_dtypes=True)
         chain = nc.gpsimd
@@ -131,12 +137,12 @@ def tile_attn_pa_kernel(tc, x_words, x_scales, w_words, w_scales, scale_param, o
         nc.scalar.activation(out=trig[:, :, 0:2, :], in_=negf[:], func=ACT.Sin, scale=-TWO_PI)
         nc.scalar.activation(out=warm[:], in_=warm[:], func=ACT.Abs_reciprocal_sqrt, bias=1.0)
 
-        nc.vector.memset(ws[V][:].bitcast(I32), 0)
         nc.vector.memset(ws[K][:].bitcast(I32), 0)
-        load_scales(ws[V], w_scales[:, :, 2 * E : 3 * E])
-        nc.sync.dma_start(out=wv[:].bitcast(I32), in_=w_words[:, :, 4 * E : 6 * E].rearrange("g p n -> p g n").bitcast(I32))
+        nc.vector.memset(ws[V][:].bitcast(I32), 0)
         load_scales(ws[K], w_scales[:, :, E : 2 * E])
         nc.sync.dma_start(out=wk[:].bitcast(I32), in_=w_words[:, :, 2 * E : 4 * E].rearrange("g p n -> p g n").bitcast(I32))
+        load_scales(ws[V], w_scales[:, :, 2 * E : 3 * E])
+        nc.sync.dma_start(out=wv[:].bitcast(I32), in_=w_words[:, :, 4 * E : 6 * E].rearrange("g p n -> p g n").bitcast(I32))
 
         nc.vector.tensor_scalar(out=trig[:, :, 2, :], in0=trig[:, :, 1, :], scalar1=-1.0, scalar2=None, op0=ALU.mult)
 
@@ -160,7 +166,7 @@ def tile_attn_pa_kernel(tc, x_words, x_scales, w_words, w_scales, scale_param, o
                 lhsT=xw[g][:, 256 * m : 256 * (m + 1)].bitcast(FP4),
                 lhsT_scale=xs[:, g, P * m : P * (m + 1)],
                 rhs=w_codes(pr, g, cb).bitcast(FP4),
-                rhs_scale=ws[pr][:, g, 512 * cb : 512 * (cb + 1)],
+                rhs_scale=(wsq[cb][:, g, :] if pr == Q else ws[pr][:, g, 512 * cb : 512 * (cb + 1)]),
                 start=(g == 0),
                 stop=(g == PASSES - 1),
             )
@@ -246,10 +252,9 @@ def tile_attn_pa_kernel(tc, x_words, x_scales, w_words, w_scales, scale_param, o
         heavy = [(pr, cb, m) for pr, cb in ((Q, 1), (K, 0), (K, 1)) for m in M_ORDER]
         light = [(V, cb, m) for cb in range(2) for m in M_ORDER]
         rest = []
-        for i in range(6):
-            rest.extend([heavy[2 * i], heavy[2 * i + 1]])
-            if i < 4:
-                rest.append(light[i])
+        rest.extend(heavy[0:4])
+        for i in range(4):
+            rest.extend([heavy[4 + 2 * i], heavy[5 + 2 * i], light[i]])
         rest.extend(light[4:7])
         for pr, cb, m in rest:
             acc = psum.tile([P, 512], F32, tag="acc", name="acc")

@@ -25,7 +25,8 @@ FLOPS = 2 * TOKENS * D_IN * 3 * E
 
 Q, K, V = 0, 1, 2
 M_ORDER = (0, 2, 1, 3)
-N_IDLE = 12
+N_IDLE = 10
+N_FIRST = 2
 ADD_SIZES = (1, 1, 2, 2, 2, 2, 2, 2, 1, 1)
 
 
@@ -53,10 +54,6 @@ def tile_attn_pa_kernel(tc, x_words, x_scales, w_words, w_scales, scale_param, o
         for pr in range(3):
             ws_pr = const.tile([P, PASSES, E], U8, name="ws%d" % pr, align_bytes=64)
             ws.append(ws_pr)
-        wsq = []
-        for cb in range(2):
-            wsq_cb = const.tile([P, PASSES, 512], U8, name="wsq%d" % cb, align_bytes=64)
-            wsq.append(wsq_cb)
         g_row = const.tile([P, E], BF16, name="g_row")
         ones = const.tile([P, P], BF16, name="ones")
         idle_rhs = const.tile([P, 512], BF16, name="idle_rhs")
@@ -97,23 +94,21 @@ def tile_attn_pa_kernel(tc, x_words, x_scales, w_words, w_scales, scale_param, o
         def load_wq(g):
             nc.sync.dma_start(out=wq[g][:].bitcast(I32), in_=w_words[g][:, 0 : 2 * E].bitcast(I32))
 
+        load_x(0)
+        load_wq(0)
         nc.gpsimd.memset(warm[:], 0.0)
-        nc.scalar.activation(out=warm[:], in_=warm[:], func=ACT.Sin)
-        nc.vector.memset(xs[:].bitcast(I32), 0)
-        nc.vector.memset(wsq[0][:].bitcast(I32), 0)
-        load_scales(xs, x_scales)
-        load_scales(wsq[0], w_scales[:, :, 0:512])
         nc.vector.memset(ones[:], 1.0)
         nc.vector.memset(idle_rhs[:], 0.0)
         nc.vector.memset(g_row[:], 0.0)
-        nc.vector.memset(wsq[1][:].bitcast(I32), 0)
-        load_x(0)
-        load_wq(0)
-        nc.sync.dma_start(out=g_row[0:1, :], in_=scale_param.rearrange("h d -> (h d)").unsqueeze(0))
+        nc.scalar.dma_start(out=g_row[0:1, :], in_=scale_param.rearrange("h d -> (h d)").unsqueeze(0))
+        nc.scalar.activation(out=warm[:], in_=warm[:], func=ACT.Sin)
+        nc.vector.memset(xs[:].bitcast(I32), 0)
+        nc.vector.memset(ws[Q][:].bitcast(I32), 0)
+        load_scales(xs, x_scales)
+        load_scales(ws[Q], w_scales[:, :, 0:E])
         for g in range(1, PASSES):
             load_x(g)
             load_wq(g)
-        load_scales(wsq[1], w_scales[:, :, 512:E])
 
         nc.gpsimd.iota(pos[:], pattern=[[P, 2]], base=0, channel_multiplier=1, allow_small_or_imprecise_dtypes=True)
         chain = nc.gpsimd
@@ -137,12 +132,12 @@ def tile_attn_pa_kernel(tc, x_words, x_scales, w_words, w_scales, scale_param, o
         nc.scalar.activation(out=trig[:, :, 0:2, :], in_=negf[:], func=ACT.Sin, scale=-TWO_PI)
         nc.scalar.activation(out=warm[:], in_=warm[:], func=ACT.Abs_reciprocal_sqrt, bias=1.0)
 
-        nc.vector.memset(ws[K][:].bitcast(I32), 0)
         nc.vector.memset(ws[V][:].bitcast(I32), 0)
-        load_scales(ws[K], w_scales[:, :, E : 2 * E])
-        nc.sync.dma_start(out=wk[:].bitcast(I32), in_=w_words[:, :, 2 * E : 4 * E].rearrange("g p n -> p g n").bitcast(I32))
+        nc.vector.memset(ws[K][:].bitcast(I32), 0)
         load_scales(ws[V], w_scales[:, :, 2 * E : 3 * E])
         nc.sync.dma_start(out=wv[:].bitcast(I32), in_=w_words[:, :, 4 * E : 6 * E].rearrange("g p n -> p g n").bitcast(I32))
+        load_scales(ws[K], w_scales[:, :, E : 2 * E])
+        nc.sync.dma_start(out=wk[:].bitcast(I32), in_=w_words[:, :, 2 * E : 4 * E].rearrange("g p n -> p g n").bitcast(I32))
 
         nc.vector.tensor_scalar(out=trig[:, :, 2, :], in0=trig[:, :, 1, :], scalar1=-1.0, scalar2=None, op0=ALU.mult)
 
@@ -166,7 +161,7 @@ def tile_attn_pa_kernel(tc, x_words, x_scales, w_words, w_scales, scale_param, o
                 lhsT=xw[g][:, 256 * m : 256 * (m + 1)].bitcast(FP4),
                 lhsT_scale=xs[:, g, P * m : P * (m + 1)],
                 rhs=w_codes(pr, g, cb).bitcast(FP4),
-                rhs_scale=(wsq[cb][:, g, :] if pr == Q else ws[pr][:, g, 512 * cb : 512 * (cb + 1)]),
+                rhs_scale=ws[pr][:, g, 512 * cb : 512 * (cb + 1)],
                 start=(g == 0),
                 stop=(g == PASSES - 1),
             )
@@ -240,21 +235,22 @@ def tile_attn_pa_kernel(tc, x_words, x_scales, w_words, w_scales, scale_param, o
                 build_tables(t, cb, g_ps[cb][:])
 
         first = []
-        for m in M_ORDER:
+        for m in M_ORDER[0:N_FIRST]:
             acc0 = psum.tile([P, 512], F32, tag="acc", name="acc0")
             first.append(acc0)
         for g in range(PASSES):
-            for i, m in enumerate(M_ORDER):
+            for i, m in enumerate(M_ORDER[0:N_FIRST]):
                 mx_pass(first[i], Q, 0, m, g)
-        for i, m in enumerate(M_ORDER):
+        for i, m in enumerate(M_ORDER[0:N_FIRST]):
             qk_epilogue(first[i], Q, 0, m)
 
         heavy = [(pr, cb, m) for pr, cb in ((Q, 1), (K, 0), (K, 1)) for m in M_ORDER]
         light = [(V, cb, m) for cb in range(2) for m in M_ORDER]
-        rest = []
-        rest.extend(heavy[0:4])
-        for i in range(4):
-            rest.extend([heavy[4 + 2 * i], heavy[5 + 2 * i], light[i]])
+        rest = [(Q, 0, m) for m in M_ORDER[N_FIRST:]]
+        for i in range(6):
+            rest.extend([heavy[2 * i], heavy[2 * i + 1]])
+            if i < 4:
+                rest.append(light[i])
         rest.extend(light[4:7])
         for pr, cb, m in rest:
             acc = psum.tile([P, 512], F32, tag="acc", name="acc")

@@ -66,12 +66,10 @@ def tile_attn_pa_kernel(tc, x_words, x_scales, w_words, w_scales, scale_param, o
         frac = const.tile([P, 4 * HALF], F32, name="frac")
         negf = const.tile([P, 2, 2, HALF], F32, name="negf")
         trig = const.tile([P, 2, 3, HALF], F32, name="trig")
-        tab_a = {}
-        tab_b = {}
+        tab = {}
         for t in range(2):
             for cb in range(2):
-                tab_a[(t, cb)] = const.tile([P, 512], F32, name="tab_a%d%d" % (t, cb))
-                tab_b[(t, cb)] = const.tile([P, 512], F32, name="tab_b%d%d" % (t, cb))
+                tab[(t, cb)] = const.tile([P, 4, 2, DH], F32, name="tab%d%d" % (t, cb))
 
         def w_codes(pr, g, cb):
             cols = slice(1024 * cb, 1024 * (cb + 1))
@@ -143,13 +141,13 @@ def tile_attn_pa_kernel(tc, x_words, x_scales, w_words, w_scales, scale_param, o
 
         def build_tables(t, cb, gain):
             nc.vector.tensor_tensor(
-                out=tab_a[(t, cb)][:].rearrange("p (a j) -> p a j", j=HALF),
-                in0=gain.rearrange("p (a j) -> p a j", j=HALF),
-                in1=trig[:, t, 0, :].unsqueeze(1).to_broadcast([P, 8, HALF]),
+                out=tab[(t, cb)][:, :, 0, :].rearrange("p h (s j) -> p h s j", j=HALF),
+                in0=gain.rearrange("p (h s j) -> p h s j", s=2, j=HALF),
+                in1=trig[:, t, 0, :].unsqueeze(1).unsqueeze(1).to_broadcast([P, 4, 2, HALF]),
                 op=ALU.mult,
             )
             nc.vector.tensor_tensor(
-                out=tab_b[(t, cb)][:].rearrange("p (h d) -> p h d", d=DH),
+                out=tab[(t, cb)][:, :, 1, :],
                 in0=gain.rearrange("p (h d) -> p h d", d=DH),
                 in1=trig[:, t, 1:3, :].rearrange("p s j -> p (s j)").unsqueeze(1).to_broadcast([P, 4, DH]),
                 op=ALU.mult,
@@ -186,35 +184,31 @@ def tile_attn_pa_kernel(tc, x_words, x_scales, w_words, w_scales, scale_param, o
                 out=rinv[:], in_=ss[:], func=ACT.Abs_reciprocal_sqrt, scale=1.0 / (DH * D_IN), bias=EPS / D_IN
             )
             if not pair:
-                t1_new = work.tile([P, 2 * 512], F32, tag="t1", bufs=4, name="t1")
-                t2_new = work.tile([P, 2 * 512], F32, tag="t2", bufs=3, name="t2")
-                pair.append((t1_new, t2_new))
-            t1, t2 = pair[0]
-            base = 512 * (len(pair) - 1)
+                prod_new = work.tile([P, 8, 2, DH], F32, tag="prod", bufs=4, name="prod")
+                pair.append(prod_new)
+            prod = pair[0]
+            base = 4 * (len(pair) - 1)
             pair.append((pr, cb, m))
             for h in range(4):
-                hs = slice(DH * h, DH * (h + 1))
-                t_cols = slice(base + DH * h, base + DH * (h + 1))
                 nc.vector.scalar_tensor_tensor(
-                    out=t1[:, t_cols], in0=acc[:, hs], scalar=rinv[:, h : h + 1], in1=tab_a[(t, cb)][:, hs], op0=ALU.mult, op1=ALU.mult
-                )
-                nc.vector.scalar_tensor_tensor(
-                    out=t2[:, t_cols], in0=acc[:, hs], scalar=rinv[:, h : h + 1], in1=tab_b[(t, cb)][:, hs], op0=ALU.mult, op1=ALU.mult
+                    out=prod[:, base + h, :, :],
+                    in0=acc[:, DH * h : DH * (h + 1)].unsqueeze(1).to_broadcast([P, 2, DH]),
+                    scalar=rinv[:, h : h + 1],
+                    in1=tab[(t, cb)][:, h, :, :],
+                    op0=ALU.mult,
+                    op1=ALU.mult,
                 )
             if len(pair) == sizes[0] + 1:
-                width = 512 * sizes[0]
+                heads = 4 * sizes[0]
                 sizes.remove(sizes[0])
                 nc.gpsimd.tensor_tensor(
-                    out=t1[:, 0:width].rearrange("p (a s j) -> p a s j", s=2, j=HALF),
-                    in0=t1[:, 0:width].rearrange("p (a s j) -> p a s j", s=2, j=HALF),
-                    in1=t2[:, 0:width].rearrange("p (a s j) -> p a s j", s=2, j=HALF)[:, :, ::-1, :],
+                    out=prod[:, 0:heads, 0, :].rearrange("p a (s j) -> p a s j", j=HALF),
+                    in0=prod[:, 0:heads, 0, :].rearrange("p a (s j) -> p a s j", j=HALF),
+                    in1=prod[:, 0:heads, 1, :].rearrange("p a (s j) -> p a s j", j=HALF)[:, :, ::-1, :],
                     op=ALU.add,
                 )
                 for i, group in enumerate(pair[1:]):
-                    nc.sync.dma_start(
-                        out=dest(group[0], group[1], group[2]),
-                        in_=t1[:, 512 * i : 512 * (i + 1)].rearrange("p (h d) -> p h d", d=DH),
-                    )
+                    nc.sync.dma_start(out=dest(group[0], group[1], group[2]), in_=prod[:, 4 * i : 4 * i + 4, 0, :])
                 pair.clear()
 
         def v_epilogue(acc, cb, m):

@@ -27,7 +27,8 @@ Q, K, V = 0, 1, 2
 M_ORDER = (0, 2, 1, 3)
 N_IDLE = 10
 N_FIRST = 2
-ADD_SIZES = (1, 1, 2, 2, 2, 2, 2, 2, 1, 1)
+ADD_SIZES = (1, 1, 2, 2, 2, 2, 2, 1, 1, 1, 1)
+ADD_ON_VECTOR = (False, False, False, False, False, False, False, False, True, False, True)
 
 
 def tile_attn_pa_kernel(tc, x_words, x_scales, w_words, w_scales, scale_param, out_q, out_k, out_v):
@@ -170,6 +171,7 @@ def tile_attn_pa_kernel(tc, x_words, x_scales, w_words, w_scales, scale_param, o
 
         pair = []
         sizes = list(ADD_SIZES)
+        on_vector = list(ADD_ON_VECTOR)
 
         def qk_epilogue(acc, pr, cb, m):
             t = m % 2
@@ -201,7 +203,9 @@ def tile_attn_pa_kernel(tc, x_words, x_scales, w_words, w_scales, scale_param, o
             if len(pair) == sizes[0] + 1:
                 heads = 4 * sizes[0]
                 sizes.remove(sizes[0])
-                nc.gpsimd.tensor_tensor(
+                adder = nc.vector if on_vector[0] else nc.gpsimd
+                on_vector.remove(on_vector[0])
+                adder.tensor_tensor(
                     out=prod[:, 0:heads, 0, :].rearrange("p a (s j) -> p a s j", j=HALF),
                     in0=prod[:, 0:heads, 0, :].rearrange("p a (s j) -> p a s j", j=HALF),
                     in1=prod[:, 0:heads, 1, :].rearrange("p a (s j) -> p a s j", j=HALF)[:, :, ::-1, :],
@@ -271,9 +275,8 @@ def tile_attn_pa_kernel(tc, x_words, x_scales, w_words, w_scales, scale_param, o
             vh = work.tile([P, 256], F32, tag="vh", bufs=2, name="vh")
             b, t = m // 2, m % 2
             dst = out_v[b, 4 * cb + 2 * half : 4 * cb + 2 * half + 2, P * t : P * (t + 1), :].rearrange("h p d -> p h d")
+            nc.scalar.copy(out=vh[:], in_=acc_h[:, 0:256])
             if half == 0:
-                nc.scalar.copy(out=vh[:], in_=acc_h[:, 0:256])
                 nc.scalar.dma_start(out=dst, in_=vh[:].rearrange("p (h d) -> p h d", d=DH))
             else:
-                nc.vector.tensor_copy(out=vh[:], in_=acc_h[:, 0:256])
                 nc.sync.dma_start(out=dst, in_=vh[:].rearrange("p (h d) -> p h d", d=DH))

@@ -175,18 +175,18 @@ def tile_attn_pa_kernel(tc, x_words, x_scales, w_words, w_scales, scale_param, o
 
         def qk_epilogue(acc, pr, cb, m):
             t = m % 2
-            ss = work.tile([P, 4], F32, tag="ss", bufs=4, name="ss")
+            ss = work.tile([P, 4], F32, tag="ss", bufs=8, name="ss")
             for h in range(4):
-                junk = work.tile([P, DH], F32, tag="junk", bufs=2, name="junk")
+                junk = work.tile([P, DH], F32, tag="junk", bufs=4, name="junk")
                 nc.scalar.activation(
                     out=junk[:], in_=acc[:, DH * h : DH * (h + 1)], func=ACT.Square, accum_out=ss[:, h : h + 1]
                 )
-            rinv = work.tile([P, 4], F32, tag="rinv", bufs=4, name="rinv")
+            rinv = work.tile([P, 4], F32, tag="rinv", bufs=8, name="rinv")
             nc.scalar.activation(
                 out=rinv[:], in_=ss[:], func=ACT.Abs_reciprocal_sqrt, scale=1.0 / (DH * D_IN), bias=EPS / D_IN
             )
             if not pair:
-                prod_new = work.tile([P, 8, 2, DH], F32, tag="prod", bufs=4, name="prod")
+                prod_new = work.tile([P, 8, 2, DH], F32, tag="prod", bufs=9, name="prod")
                 pair.append(prod_new)
             prod = pair[0]
             base = 4 * (len(pair) - 1)
@@ -216,7 +216,7 @@ def tile_attn_pa_kernel(tc, x_words, x_scales, w_words, w_scales, scale_param, o
                 pair.clear()
 
         def v_epilogue(acc, cb, m):
-            vo = work.tile([P, 512], F32, tag="vo", bufs=4, name="vo")
+            vo = work.tile([P, 512], F32, tag="vo", bufs=7, name="vo")
             nc.scalar.copy(out=vo[:], in_=acc[:])
             nc.scalar.dma_start(out=dest(V, cb, m), in_=vo[:].rearrange("p (h d) -> p h d", d=DH))
 

@@ -247,9 +247,9 @@ def tile_attn_pa_kernel(tc, x_words, x_scales, w_words, w_scales, scale_param, o
         rest = [(Q, 0, m) for m in M_ORDER[N_FIRST:]]
         for i in range(6):
             rest.extend([heavy[2 * i], heavy[2 * i + 1]])
-            if i < 4:
+            if i < 5:
                 rest.append(light[i])
-        rest.extend(light[4:7])
+        rest.extend(light[5:7])
         for pr, cb, m in rest:
             acc = psum.tile([P, 512], F32, tag="acc", name="acc")
             for g in range(PASSES):

@@ -110,12 +110,9 @@ def tile_attn_pa_kernel(tc, x_words, x_scales, w_words, w_scales, scale_param, o
             load_wq(g)
 
         nc.gpsimd.iota(pos[:], pattern=[[P, 2]], base=0, channel_multiplier=1, allow_small_or_imprecise_dtypes=True)
-        chain = nc.gpsimd
-        chain.memset(freq[:, 0:1], 1.0)
+        nc.vector.memset(freq[:, 0:1], 1.0)
         for w in (1, 2, 4, 8, 16, 32):
-            chain.tensor_scalar(
-                out=freq[:, w : 2 * w], in0=freq[:, 0:w], scalar1=RATIO**w, scalar2=0.0, op0=ALU.mult, op1=ALU.add
-            )
+            nc.vector.tensor_scalar(out=freq[:, w : 2 * w], in0=freq[:, 0:w], scalar1=RATIO**w, scalar2=None, op0=ALU.mult)
         nc.vector.tensor_scalar(out=pos_turns[:], in0=pos[:], scalar1=1.0 / TWO_PI, scalar2=None, op0=ALU.mult)
         for t in range(2):
             for s, off in enumerate((0.25, 0.0)):
@@ -228,9 +225,9 @@ def tile_attn_pa_kernel(tc, x_words, x_scales, w_words, w_scales, scale_param, o
             g_half = psum.tile([P, 512], F32, tag="acc", name="g_half%d" % cb)
             nc.tensor.matmul(out=g_half[:], lhsT=ones[:], rhs=g_row[:, 512 * cb : 512 * (cb + 1)], start=True, stop=True)
             g_ps.append(g_half)
-        for cb in range(2):
-            for t in range(2):
-                build_tables(t, cb, g_ps[cb][:])
+        build_tables(0, 0, g_ps[0][:])
+        build_tables(1, 0, g_ps[0][:])
+        build_tables(0, 1, g_ps[1][:])
 
         first = []
         for m in M_ORDER[0:N_FIRST]:
@@ -241,6 +238,7 @@ def tile_attn_pa_kernel(tc, x_words, x_scales, w_words, w_scales, scale_param, o
                 mx_pass(first[i], Q, 0, m, g)
         for i, m in enumerate(M_ORDER[0:N_FIRST]):
             qk_epilogue(first[i], Q, 0, m)
+        build_tables(1, 1, g_ps[1][:])
 
         heavy = [(pr, cb, m) for pr, cb in ((Q, 1), (K, 0), (K, 1)) for m in M_ORDER]
         light = [(V, cb, m) for cb in range(2) for m in M_ORDER]

@@ -44,16 +44,16 @@ def tile_attn_pa_kernel(tc, x_words, x_scales, w_words, w_scales, scale_param, o
         xw = []
         wq = []
         for g in range(PASSES):
-            xw_g = const.tile([P, 2 * TOKENS], U8, name="xw%d" % g, align_bytes=64)
+            xw_g = const.tile([P, 2 * TOKENS], U8, name="xw%d" % g, align_bytes=256)
             xw.append(xw_g)
-            wq_g = const.tile([P, 2 * E], U8, name="wq%d" % g, align_bytes=64)
+            wq_g = const.tile([P, 2 * E], U8, name="wq%d" % g, align_bytes=256)
             wq.append(wq_g)
-        xs = const.tile([P, PASSES, TOKENS], U8, name="xs", align_bytes=64)
-        wk = const.tile([P, PASSES, 2 * E], U8, name="wk", align_bytes=64)
-        wv = const.tile([P, PASSES, 2 * E], U8, name="wv", align_bytes=64)
+        xs = const.tile([P, PASSES, TOKENS], U8, name="xs", align_bytes=256)
+        wk = const.tile([P, PASSES, 2 * E], U8, name="wk", align_bytes=256)
+        wv = const.tile([P, PASSES, 2 * E], U8, name="wv", align_bytes=256)
         ws = []
         for pr in range(3):
-            ws_pr = const.tile([P, PASSES, E], U8, name="ws%d" % pr, align_bytes=64)
+            ws_pr = const.tile([P, PASSES, E], U8, name="ws%d" % pr, align_bytes=256)
             ws.append(ws_pr)
         g_row = const.tile([P, E], BF16, name="g_row")
         ones = const.tile([P, P], BF16, name="ones")
@@ -183,7 +183,7 @@ def tile_attn_pa_kernel(tc, x_words, x_scales, w_words, w_scales, scale_param, o
                 out=rinv[:], in_=ss[:], func=ACT.Abs_reciprocal_sqrt, scale=1.0 / (DH * D_IN), bias=EPS / D_IN
             )
             if not pair:
-                prod_new = work.tile([P, 8, 2, DH], F32, tag="prod", bufs=9, name="prod")
+                prod_new = work.tile([P, 8, 2, DH], F32, tag="prod", bufs=9, name="prod", align_bytes=256)
                 pair.append(prod_new)
             prod = pair[0]
             base = 4 * (len(pair) - 1)
@@ -213,7 +213,7 @@ def tile_attn_pa_kernel(tc, x_words, x_scales, w_words, w_scales, scale_param, o
                 pair.clear()
 
         def v_epilogue(acc, cb, m):
-            vo = work.tile([P, 512], F32, tag="vo", bufs=7, name="vo")
+            vo = work.tile([P, 512], F32, tag="vo", bufs=7, name="vo", align_bytes=256)
             nc.scalar.copy(out=vo[:], in_=acc[:])
             nc.scalar.dma_start(out=dest(V, cb, m), in_=vo[:].rearrange("p (h d) -> p h d", d=DH))
 
@@ -270,7 +270,7 @@ def tile_attn_pa_kernel(tc, x_words, x_scales, w_words, w_scales, scale_param, o
                     start=(g == 0),
                     stop=(g == PASSES - 1),
                 )
-            vh = work.tile([P, 256], F32, tag="vh", bufs=2, name="vh")
+            vh = work.tile([P, 256], F32, tag="vh", bufs=2, name="vh", align_bytes=256)
             b, t = m // 2, m % 2
             dst = out_v[b, 4 * cb + 2 * half : 4 * cb + 2 * half + 2, P * t : P * (t + 1), :].rearrange("h p d -> p h d")
             nc.scalar.copy(out=vh[:], in_=acc_h[:, 0:256])

@@ -25,8 +25,9 @@ FLOPS = 2 * TOKENS * D_IN * 3 * E
 
 Q, K, V = 0, 1, 2
 M_ORDER = (0, 2, 1, 3)
-N_IDLE = 10
-N_FIRST = 2
+N_IDLE_A = 4
+N_IDLE_B = 5
+V_AMONG = 5
 ADD_SIZES = (1, 1, 2, 2, 2, 2, 2, 1, 1, 1, 1)
 ADD_ON_VECTOR = (False, False, False, False, False, False, False, False, True, False, True)
 
@@ -42,12 +43,13 @@ def tile_attn_pa_kernel(tc, x_words, x_scales, w_words, w_scales, scale_param, o
         ctx.enter_context(tc.manual_schedule())
 
         xw = []
-        wq = []
+        wqa = []
         for g in range(PASSES):
             xw_g = const.tile([P, 2 * TOKENS], U8, name="xw%d" % g, align_bytes=256)
             xw.append(xw_g)
-            wq_g = const.tile([P, 2 * E], U8, name="wq%d" % g, align_bytes=256)
-            wq.append(wq_g)
+            wqa_g = const.tile([P, E], U8, name="wqa%d" % g, align_bytes=256)
+            wqa.append(wqa_g)
+        wqb = const.tile([P, PASSES, E], U8, name="wqb", align_bytes=256)
         xs = const.tile([P, PASSES, TOKENS], U8, name="xs", align_bytes=256)
         wk = const.tile([P, PASSES, 2 * E], U8, name="wk", align_bytes=256)
         wv = const.tile([P, PASSES, 2 * E], U8, name="wv", align_bytes=256)
@@ -55,13 +57,12 @@ def tile_attn_pa_kernel(tc, x_words, x_scales, w_words, w_scales, scale_param, o
         for pr in range(3):
             ws_pr = const.tile([P, PASSES, E], U8, name="ws%d" % pr, align_bytes=256)
             ws.append(ws_pr)
-        g_row = const.tile([P, E], BF16, name="g_row")
+        g_row = const.tile([P, E], BF16, name="g_row", align_bytes=256)
+        g_one = const.tile([1, E], BF16, name="g_one", align_bytes=256)
         ones = const.tile([P, P], BF16, name="ones")
         idle_rhs = const.tile([P, 512], BF16, name="idle_rhs")
         warm = const.tile([P, 1], F32, name="warm")
         pos = const.tile([P, 2], F32, name="pos")
-        pos_turns = const.tile([P, 2], F32, name="pos_turns")
-        freq = const.tile([P, HALF], F32, name="freq")
         turns = const.tile([P, 2, 2, HALF], F32, name="turns")
         whole = const.tile([P, 4 * HALF], I32, name="whole")
         frac = const.tile([P, 4 * HALF], F32, name="frac")
@@ -75,7 +76,9 @@ def tile_attn_pa_kernel(tc, x_words, x_scales, w_words, w_scales, scale_param, o
         def w_codes(pr, g, cb):
             cols = slice(1024 * cb, 1024 * (cb + 1))
             if pr == Q:
-                return wq[g][:, cols]
+                if cb == 0:
+                    return wqa[g][:, :]
+                return wqb[:, g, :]
             if pr == K:
                 return wk[:, g, cols]
             return wv[:, g, cols]
@@ -90,35 +93,33 @@ def tile_attn_pa_kernel(tc, x_words, x_scales, w_words, w_scales, scale_param, o
         def load_x(g):
             nc.sync.dma_start(out=xw[g][:].bitcast(I32), in_=x_words[g].bitcast(I32))
 
-        def load_wq(g):
-            nc.sync.dma_start(out=wq[g][:].bitcast(I32), in_=w_words[g][:, 0 : 2 * E].bitcast(I32))
+        def load_wqa(g):
+            nc.sync.dma_start(out=wqa[g][:].bitcast(I32), in_=w_words[g][:, 0:E].bitcast(I32))
 
+        nc.sync.dma_start(out=g_one[:], in_=scale_param.rearrange("h d -> (h d)").unsqueeze(0))
         load_x(0)
-        load_wq(0)
+        load_wqa(0)
         nc.gpsimd.memset(warm[:], 0.0)
+        nc.gpsimd.iota(pos[:], pattern=[[P, 2]], base=0, channel_multiplier=1, allow_small_or_imprecise_dtypes=True)
+        nc.vector.memset(xs[:].bitcast(I32), 0)
         nc.vector.memset(ones[:], 1.0)
         nc.vector.memset(idle_rhs[:], 0.0)
-        nc.vector.memset(g_row[:], 0.0)
-        nc.scalar.dma_start(out=g_row[0:1, :], in_=scale_param.rearrange("h d -> (h d)").unsqueeze(0))
-        nc.scalar.activation(out=warm[:], in_=warm[:], func=ACT.Sin)
-        nc.vector.memset(xs[:].bitcast(I32), 0)
         nc.vector.memset(ws[Q][:].bitcast(I32), 0)
+        nc.vector.memset(g_row[:], 0.0)
         load_scales(xs, x_scales)
         load_scales(ws[Q], w_scales[:, :, 0:E])
         for g in range(1, PASSES):
             load_x(g)
-            load_wq(g)
+            load_wqa(g)
+        nc.sync.dma_start(out=wqb[:].bitcast(I32), in_=w_words[:, :, E : 2 * E].rearrange("g p n -> p g n").bitcast(I32))
+        nc.vector.tensor_copy(out=g_row[0:1, :], in_=g_one[:])
+        nc.vector.memset(ws[V][:].bitcast(I32), 0)
 
-        nc.gpsimd.iota(pos[:], pattern=[[P, 2]], base=0, channel_multiplier=1, allow_small_or_imprecise_dtypes=True)
-        nc.vector.memset(freq[:, 0:1], 1.0)
+        nc.scalar.activation(out=warm[:], in_=warm[:], func=ACT.Sin)
+        nc.scalar.activation(out=turns[:, :, 1, 0:1], in_=pos[:].unsqueeze(2), func=ACT.Copy, scale=1.0 / TWO_PI)
         for w in (1, 2, 4, 8, 16, 32):
-            nc.vector.tensor_scalar(out=freq[:, w : 2 * w], in0=freq[:, 0:w], scalar1=RATIO**w, scalar2=None, op0=ALU.mult)
-        nc.vector.tensor_scalar(out=pos_turns[:], in0=pos[:], scalar1=1.0 / TWO_PI, scalar2=None, op0=ALU.mult)
-        for t in range(2):
-            for s, off in enumerate((0.25, 0.0)):
-                nc.vector.tensor_scalar(
-                    out=turns[:, t, s, :], in0=freq[:], scalar1=pos_turns[:, t : t + 1], scalar2=off, op0=ALU.mult, op1=ALU.add
-                )
+            nc.scalar.activation(out=turns[:, :, 1, w : 2 * w], in_=turns[:, :, 1, 0:w], func=ACT.Copy, scale=RATIO**w)
+        nc.scalar.activation(out=turns[:, :, 0, :], in_=turns[:, :, 1, :], func=ACT.Copy, bias=0.25)
         turns_flat = turns[:].rearrange("p t s j -> p (t s j)")
         nc.vector.tensor_copy(out=whole[:], in_=turns_flat)
         nc.vector.tensor_tensor(out=frac[:], in0=turns_flat, in1=whole[:], op=ALU.subtract)
@@ -126,18 +127,20 @@ def tile_attn_pa_kernel(tc, x_words, x_scales, w_words, w_scales, scale_param, o
             out=negf[:].rearrange("p t s j -> p (t s j)"), in0=frac[:], scalar=0.5, in1=frac[:], op0=ALU.is_gt, op1=ALU.subtract
         )
         nc.scalar.activation(out=trig[:, :, 0:2, :], in_=negf[:], func=ACT.Sin, scale=-TWO_PI)
+        nc.scalar.activation(out=trig[:, :, 2, :], in_=negf[:, :, 1, :], func=ACT.Sin, scale=TWO_PI)
         nc.scalar.activation(out=warm[:], in_=warm[:], func=ACT.Abs_reciprocal_sqrt, bias=1.0)
 
-        nc.vector.memset(ws[V][:].bitcast(I32), 0)
         nc.vector.memset(ws[K][:].bitcast(I32), 0)
         load_scales(ws[V], w_scales[:, :, 2 * E : 3 * E])
         nc.sync.dma_start(out=wv[:].bitcast(I32), in_=w_words[:, :, 4 * E : 6 * E].rearrange("g p n -> p g n").bitcast(I32))
         load_scales(ws[K], w_scales[:, :, E : 2 * E])
         nc.sync.dma_start(out=wk[:].bitcast(I32), in_=w_words[:, :, 2 * E : 4 * E].rearrange("g p n -> p g n").bitcast(I32))
 
-        nc.vector.tensor_scalar(out=trig[:, :, 2, :], in0=trig[:, :, 1, :], scalar1=-1.0, scalar2=None, op0=ALU.mult)
+        built = []
 
-        def build_tables(t, cb, gain):
+        def build_tables(t, cb):
+            gain = g_ps[cb][:]
+            built.append((t, cb))
             nc.vector.tensor_tensor(
                 out=tab[(t, cb)][:, :, 0, :].rearrange("p h (s j) -> p h s j", j=HALF),
                 in0=gain.rearrange("p (h s j) -> p h s j", s=2, j=HALF),
@@ -182,6 +185,8 @@ def tile_attn_pa_kernel(tc, x_words, x_scales, w_words, w_scales, scale_param, o
             nc.scalar.activation(
                 out=rinv[:], in_=ss[:], func=ACT.Abs_reciprocal_sqrt, scale=1.0 / (DH * D_IN), bias=EPS / D_IN
             )
+            if (t, cb) not in built:
+                build_tables(t, cb)
             if not pair:
                 prod_new = work.tile([P, 8, 2, DH], F32, tag="prod", bufs=9, name="prod", align_bytes=256)
                 pair.append(prod_new)
@@ -218,36 +223,43 @@ def tile_attn_pa_kernel(tc, x_words, x_scales, w_words, w_scales, scale_param, o
             nc.scalar.dma_start(out=dest(V, cb, m), in_=vo[:].rearrange("p (h d) -> p h d", d=DH))
 
         idle_ps = psum.tile([P, 512], F32, tag="acc", name="idle_ps")
-        for i in range(N_IDLE):
-            nc.tensor.matmul(out=idle_ps[:], lhsT=ones[:], rhs=idle_rhs[:], start=True, stop=True)
+        first = []
+        for m in M_ORDER:
+            acc0 = psum.tile([P, 512], F32, tag="acc", name="acc0")
+            first.append(acc0)
         g_ps = []
         for cb in range(2):
             g_half = psum.tile([P, 512], F32, tag="acc", name="g_half%d" % cb)
-            nc.tensor.matmul(out=g_half[:], lhsT=ones[:], rhs=g_row[:, 512 * cb : 512 * (cb + 1)], start=True, stop=True)
             g_ps.append(g_half)
-        build_tables(0, 0, g_ps[0][:])
-        build_tables(1, 0, g_ps[0][:])
-        build_tables(0, 1, g_ps[1][:])
 
-        first = []
-        for m in M_ORDER[0:N_FIRST]:
-            acc0 = psum.tile([P, 512], F32, tag="acc", name="acc0")
-            first.append(acc0)
-        for g in range(PASSES):
-            for i, m in enumerate(M_ORDER[0:N_FIRST]):
-                mx_pass(first[i], Q, 0, m, g)
-        for i, m in enumerate(M_ORDER[0:N_FIRST]):
+        for i in range(N_IDLE_A):
+            nc.tensor.matmul(out=idle_ps[:], lhsT=ones[:], rhs=idle_rhs[:], start=True, stop=True)
+        for cb in range(2):
+            nc.tensor.matmul(out=g_ps[cb][:], lhsT=ones[:], rhs=g_row[:, 512 * cb : 512 * (cb + 1)], start=True, stop=True)
+        for i in range(N_IDLE_B):
+            nc.tensor.matmul(out=idle_ps[:], lhsT=ones[:], rhs=idle_rhs[:], start=True, stop=True)
+        build_tables(0, 0)
+        build_tables(1, 0)
+
+        for i, m in enumerate(M_ORDER):
+            mx_pass(first[i], Q, 0, m, 0)
+        for g in range(1, PASSES):
+            for i in range(2):
+                mx_pass(first[i], Q, 0, M_ORDER[i], g)
+        for i in range(2, 4):
+            for g in range(1, PASSES):
+                mx_pass(first[i], Q, 0, M_ORDER[i], g)
+        for i, m in enumerate(M_ORDER):
             qk_epilogue(first[i], Q, 0, m)
-        build_tables(1, 1, g_ps[1][:])
 
         heavy = [(pr, cb, m) for pr, cb in ((Q, 1), (K, 0), (K, 1)) for m in M_ORDER]
         light = [(V, cb, m) for cb in range(2) for m in M_ORDER]
-        rest = [(Q, 0, m) for m in M_ORDER[N_FIRST:]]
+        rest = []
         for i in range(6):
             rest.extend([heavy[2 * i], heavy[2 * i + 1]])
-            if i < 5:
+            if i < V_AMONG:
                 rest.append(light[i])
-        rest.extend(light[5:7])
+        rest.extend(light[V_AMONG:7])
         for pr, cb, m in rest:
             acc = psum.tile([P, 512], F32, tag="acc", name="acc")
             for g in range(PASSES):

@@ -101,25 +101,39 @@ def tile_attn_pa_kernel(tc, x_words, x_scales, w_words, w_scales, scale_param, o
         load_wqa(0)
         nc.gpsimd.memset(warm[:], 0.0)
         nc.gpsimd.iota(pos[:], pattern=[[P, 2]], base=0, channel_multiplier=1, allow_small_or_imprecise_dtypes=True)
+
+        def double(w):
+            nc.vector.tensor_scalar(
+                out=turns[:, :, 1, w : 2 * w], in0=turns[:, :, 1, 0:w], scalar1=RATIO**w, scalar2=None, op0=ALU.mult
+            )
+
         nc.vector.memset(xs[:].bitcast(I32), 0)
+        nc.vector.tensor_scalar(
+            out=turns[:, :, 1, 0:1], in0=pos[:].unsqueeze(2), scalar1=1.0 / TWO_PI, scalar2=None, op0=ALU.mult
+        )
         nc.vector.memset(ones[:], 1.0)
+        double(1)
         nc.vector.memset(idle_rhs[:], 0.0)
+        double(2)
         nc.vector.memset(ws[Q][:].bitcast(I32), 0)
+        double(4)
         nc.vector.memset(g_row[:], 0.0)
+        double(8)
+        nc.vector.tensor_copy(out=g_row[0:1, :], in_=g_one[:])
         load_scales(xs, x_scales)
         load_scales(ws[Q], w_scales[:, :, 0:E])
         for g in range(1, PASSES):
             load_x(g)
             load_wqa(g)
         nc.sync.dma_start(out=wqb[:].bitcast(I32), in_=w_words[:, :, E : 2 * E].rearrange("g p n -> p g n").bitcast(I32))
-        nc.vector.tensor_copy(out=g_row[0:1, :], in_=g_one[:])
         nc.vector.memset(ws[V][:].bitcast(I32), 0)
+        double(16)
+        nc.vector.memset(ws[K][:, 0:2, :].bitcast(I32), 0)
+        double(32)
+        nc.vector.memset(ws[K][:, 2:4, :].bitcast(I32), 0)
+        nc.vector.tensor_scalar(out=turns[:, :, 0, :], in0=turns[:, :, 1, :], scalar1=0.25, scalar2=None, op0=ALU.add)
 
         nc.scalar.activation(out=warm[:], in_=warm[:], func=ACT.Sin)
-        nc.scalar.activation(out=turns[:, :, 1, 0:1], in_=pos[:].unsqueeze(2), func=ACT.Copy, scale=1.0 / TWO_PI)
-        for w in (1, 2, 4, 8, 16, 32):
-            nc.scalar.activation(out=turns[:, :, 1, w : 2 * w], in_=turns[:, :, 1, 0:w], func=ACT.Copy, scale=RATIO**w)
-        nc.scalar.activation(out=turns[:, :, 0, :], in_=turns[:, :, 1, :], func=ACT.Copy, bias=0.25)
         turns_flat = turns[:].rearrange("p t s j -> p (t s j)")
         nc.vector.tensor_copy(out=whole[:], in_=turns_flat)
         nc.vector.tensor_tensor(out=frac[:], in0=turns_flat, in1=whole[:], op=ALU.subtract)
@@ -130,7 +144,6 @@ def tile_attn_pa_kernel(tc, x_words, x_scales, w_words, w_scales, scale_param, o
         nc.scalar.activation(out=trig[:, :, 2, :], in_=negf[:, :, 1, :], func=ACT.Sin, scale=TWO_PI)
         nc.scalar.activation(out=warm[:], in_=warm[:], func=ACT.Abs_reciprocal_sqrt, bias=1.0)
 
-        nc.vector.memset(ws[K][:].bitcast(I32), 0)
         load_scales(ws[V], w_scales[:, :, 2 * E : 3 * E])
         nc.sync.dma_start(out=wv[:].bitcast(I32), in_=w_words[:, :, 4 * E : 6 * E].rearrange("g p n -> p g n").bitcast(I32))
         load_scales(ws[K], w_scales[:, :, E : 2 * E])
@@ -240,6 +253,7 @@ def tile_attn_pa_kernel(tc, x_words, x_scales, w_words, w_scales, scale_param, o
             nc.tensor.matmul(out=idle_ps[:], lhsT=ones[:], rhs=idle_rhs[:], start=True, stop=True)
         build_tables(0, 0)
         build_tables(1, 0)
+        build_tables(0, 1)
 
         for i, m in enumerate(M_ORDER):
             mx_pass(first[i], Q, 0, m, 0)

@@ -84,10 +84,10 @@ def tile_attn_pa_kernel(tc, x_words, x_scales, w_words, w_scales, scale_param, o
             return wv[:, g, cols]
 
         def load_scales(plane, src):
-            for quad in range(4):
+            for r in range(4):
                 nc.sync.dma_start(
-                    out=plane[32 * quad : 32 * quad + 4, :, :].bitcast(I32),
-                    in_=src[:, 4 * quad : 4 * quad + 4, :].rearrange("g r n -> r g n").bitcast(I32),
+                    out=plane[r : P : 32, :, :].bitcast(I32),
+                    in_=src[:, r : 16 : 4, :].rearrange("g q n -> q g n").bitcast(I32),
                 )
 
         def load_x(g):
@@ -107,7 +107,7 @@ def tile_attn_pa_kernel(tc, x_words, x_scales, w_words, w_scales, scale_param, o
                 out=turns[:, :, 1, w : 2 * w], in0=turns[:, :, 1, 0:w], scalar1=RATIO**w, scalar2=None, op0=ALU.mult
             )
 
-        nc.vector.memset(xs[:].bitcast(I32), 0)
+        nc.vector.memset(ws[Q][:].bitcast(I32), 0)
         nc.vector.tensor_scalar(
             out=turns[:, :, 1, 0:1], in0=pos[:].unsqueeze(2), scalar1=1.0 / TWO_PI, scalar2=None, op0=ALU.mult
         )
@@ -115,13 +115,13 @@ def tile_attn_pa_kernel(tc, x_words, x_scales, w_words, w_scales, scale_param, o
         double(1)
         nc.vector.memset(idle_rhs[:], 0.0)
         double(2)
-        nc.vector.memset(ws[Q][:].bitcast(I32), 0)
+        nc.vector.memset(xs[:].bitcast(I32), 0)
         double(4)
         nc.vector.memset(g_row[:], 0.0)
         double(8)
         nc.vector.tensor_copy(out=g_row[0:1, :], in_=g_one[:])
-        load_scales(xs, x_scales)
         load_scales(ws[Q], w_scales[:, :, 0:E])
+        load_scales(xs, x_scales)
         for g in range(1, PASSES):
             load_x(g)
             load_wqa(g)

@@ -26,7 +26,7 @@ FLOPS = 2 * TOKENS * D_IN * 3 * E
 Q, K, V = 0, 1, 2
 M_ORDER = (0, 2, 1, 3)
 N_IDLE_A = 4
-N_IDLE_B = 5
+N_IDLE_B = 3
 V_AMONG = 5
 ADD_SIZES = (1, 1, 2, 2, 2, 2, 2, 1, 1, 1, 1)
 ADD_ON_VECTOR = (False, False, False, False, False, False, False, False, True, False, True)

from contextlib import ExitStack

import concourse.mybir as mybir

F32 = mybir.dt.float32
BF16 = mybir.dt.bfloat16
U8 = mybir.dt.uint8
I32 = mybir.dt.int32
FP4 = mybir.dt.float4_e2m1fn_x4
ALU = mybir.AluOpType
ACT = mybir.ActivationFunctionType

P = 128
PASSES = 4
TOKENS = 512
D_IN = 2048
E = 1024
DH = 128
HALF = 64
EPS = 1e-6
TWO_PI = 6.283185307179586
RATIO = 10000.0 ** (-1.0 / 64.0)

FLOPS = 2 * TOKENS * D_IN * 3 * E

Q, K, V = 0, 1, 2
M_ORDER = (0, 2, 1, 3)
N_IDLE_A = 4
N_IDLE_B = 3
V_AMONG = 5
ADD_SIZES = (1, 1, 2, 2, 2, 2, 2, 1, 1, 1, 1)
ADD_ON_VECTOR = (False, False, False, False, False, False, False, False, True, False, True)


def tile_attn_pa_kernel(tc, x_words, x_scales, w_words, w_scales, scale_param, out_q, out_k, out_v):
    nc = tc.nc
    outs = (out_q, out_k, out_v)

    with ExitStack() as ctx:
        const = ctx.enter_context(tc.tile_pool(name="const", bufs=1))
        work = ctx.enter_context(tc.tile_pool(name="work", bufs=4))
        psum = ctx.enter_context(tc.psum_pool(name="psum", bufs=8))
        ctx.enter_context(tc.manual_schedule())

        xw = []
        wqa = []
        for g in range(PASSES):
            xw_g = const.tile([P, 2 * TOKENS], U8, name="xw%d" % g, align_bytes=256)
            xw.append(xw_g)
            wqa_g = const.tile([P, E], U8, name="wqa%d" % g, align_bytes=256)
            wqa.append(wqa_g)
        wqb = const.tile([P, PASSES, E], U8, name="wqb", align_bytes=256)
        xs = const.tile([P, PASSES, TOKENS], U8, name="xs", align_bytes=256)
        wk = const.tile([P, PASSES, 2 * E], U8, name="wk", align_bytes=256)
        wv = const.tile([P, PASSES, 2 * E], U8, name="wv", align_bytes=256)
        ws = []
        for pr in range(3):
            ws_pr = const.tile([P, PASSES, E], U8, name="ws%d" % pr, align_bytes=256)
            ws.append(ws_pr)
        g_row = const.tile([P, E], BF16, name="g_row", align_bytes=256)
        g_one = const.tile([1, E], BF16, name="g_one", align_bytes=256)
        ones = const.tile([P, P], BF16, name="ones")
        idle_rhs = const.tile([P, 512], BF16, name="idle_rhs")
        warm = const.tile([P, 1], F32, name="warm")
        pos = const.tile([P, 2], F32, name="pos")
        turns = const.tile([P, 2, 2, HALF], F32, name="turns")
        whole = const.tile([P, 4 * HALF], I32, name="whole")
        frac = const.tile([P, 4 * HALF], F32, name="frac")
        negf = const.tile([P, 2, 2, HALF], F32, name="negf")
        trig = const.tile([P, 2, 3, HALF], F32, name="trig")
        tab = {}
        for t in range(2):
            for cb in range(2):
                tab[(t, cb)] = const.tile([P, 4, 2, DH], F32, name="tab%d%d" % (t, cb))

        def w_codes(pr, g, cb):
            cols = slice(1024 * cb, 1024 * (cb + 1))
            if pr == Q:
                if cb == 0:
                    return wqa[g][:, :]
                return wqb[:, g, :]
            if pr == K:
                return wk[:, g, cols]
            return wv[:, g, cols]

        def load_scales(plane, src):
            for r in range(4):
                nc.sync.dma_start(
                    out=plane[r : P : 32, :, :].bitcast(I32),
                    in_=src[:, r : 16 : 4, :].rearrange("g q n -> q g n").bitcast(I32),
                )

        def load_x(g):
            nc.sync.dma_start(out=xw[g][:].bitcast(I32), in_=x_words[g].bitcast(I32))

        def load_wqa(g):
            nc.sync.dma_start(out=wqa[g][:].bitcast(I32), in_=w_words[g][:, 0:E].bitcast(I32))

        nc.sync.dma_start(out=g_one[:], in_=scale_param.rearrange("h d -> (h d)").unsqueeze(0))
        load_x(0)
        load_wqa(0)
        nc.gpsimd.memset(warm[:], 0.0)
        nc.gpsimd.iota(pos[:], pattern=[[P, 2]], base=0, channel_multiplier=1, allow_small_or_imprecise_dtypes=True)

        def double(w):
            nc.vector.tensor_scalar(
                out=turns[:, :, 1, w : 2 * w], in0=turns[:, :, 1, 0:w], scalar1=RATIO**w, scalar2=None, op0=ALU.mult
            )

        nc.vector.memset(ws[Q][:].bitcast(I32), 0)
        nc.vector.tensor_scalar(
            out=turns[:, :, 1, 0:1], in0=pos[:].unsqueeze(2), scalar1=1.0 / TWO_PI, scalar2=None, op0=ALU.mult
        )
        nc.vector.memset(ones[:], 1.0)
        double(1)
        nc.vector.memset(idle_rhs[:], 0.0)
        double(2)
        nc.vector.memset(xs[:].bitcast(I32), 0)
        double(4)
        nc.vector.memset(g_row[:], 0.0)
        double(8)
        nc.vector.tensor_copy(out=g_row[0:1, :], in_=g_one[:])
        load_scales(ws[Q], w_scales[:, :, 0:E])
        load_scales(xs, x_scales)
        for g in range(1, PASSES):
            load_x(g)
            load_wqa(g)
        nc.sync.dma_start(out=wqb[:].bitcast(I32), in_=w_words[:, :, E : 2 * E].rearrange("g p n -> p g n").bitcast(I32))
        nc.vector.memset(ws[V][:].bitcast(I32), 0)
        double(16)
        nc.vector.memset(ws[K][:, 0:2, :].bitcast(I32), 0)
        double(32)
        nc.vector.memset(ws[K][:, 2:4, :].bitcast(I32), 0)
        nc.vector.tensor_scalar(out=turns[:, :, 0, :], in0=turns[:, :, 1, :], scalar1=0.25, scalar2=None, op0=ALU.add)

        nc.scalar.activation(out=warm[:], in_=warm[:], func=ACT.Sin)
        turns_flat = turns[:].rearrange("p t s j -> p (t s j)")
        nc.vector.tensor_copy(out=whole[:], in_=turns_flat)
        nc.vector.tensor_tensor(out=frac[:], in0=turns_flat, in1=whole[:], op=ALU.subtract)
        nc.vector.scalar_tensor_tensor(
            out=negf[:].rearrange("p t s j -> p (t s j)"), in0=frac[:], scalar=0.5, in1=frac[:], op0=ALU.is_gt, op1=ALU.subtract
        )
        nc.scalar.activation(out=trig[:, :, 0:2, :], in_=negf[:], func=ACT.Sin, scale=-TWO_PI)
        nc.scalar.activation(out=trig[:, :, 2, :], in_=negf[:, :, 1, :], func=ACT.Sin, scale=TWO_PI)
        nc.scalar.activation(out=warm[:], in_=warm[:], func=ACT.Abs_reciprocal_sqrt, bias=1.0)

        load_scales(ws[V], w_scales[:, :, 2 * E : 3 * E])
        nc.sync.dma_start(out=wv[:].bitcast(I32), in_=w_words[:, :, 4 * E : 6 * E].rearrange("g p n -> p g n").bitcast(I32))
        load_scales(ws[K], w_scales[:, :, E : 2 * E])
        nc.sync.dma_start(out=wk[:].bitcast(I32), in_=w_words[:, :, 2 * E : 4 * E].rearrange("g p n -> p g n").bitcast(I32))

        built = []

        def build_tables(t, cb):
            gain = g_ps[cb][:]
            built.append((t, cb))
            nc.vector.tensor_tensor(
                out=tab[(t, cb)][:, :, 0, :].rearrange("p h (s j) -> p h s j", j=HALF),
                in0=gain.rearrange("p (h s j) -> p h s j", s=2, j=HALF),
                in1=trig[:, t, 0, :].unsqueeze(1).unsqueeze(1).to_broadcast([P, 4, 2, HALF]),
                op=ALU.mult,
            )
            nc.vector.tensor_tensor(
                out=tab[(t, cb)][:, :, 1, :],
                in0=gain.rearrange("p (h d) -> p h d", d=DH),
                in1=trig[:, t, 1:3, :].rearrange("p s j -> p (s j)").unsqueeze(1).to_broadcast([P, 4, DH]),
                op=ALU.mult,
            )

        def mx_pass(acc, pr, cb, m, g):
            nc.tensor.matmul_mx(
                out=acc[:],
                lhsT=xw[g][:, 256 * m : 256 * (m + 1)].bitcast(FP4),
                lhsT_scale=xs[:, g, P * m : P * (m + 1)],
                rhs=w_codes(pr, g, cb).bitcast(FP4),
                rhs_scale=ws[pr][:, g, 512 * cb : 512 * (cb + 1)],
                start=(g == 0),
                stop=(g == PASSES - 1),
            )

        def dest(pr, cb, m):
            b, t = m // 2, m % 2
            return outs[pr][b, 4 * cb : 4 * cb + 4, P * t : P * (t + 1), :].rearrange("h p d -> p h d")

        pair = []
        sizes = list(ADD_SIZES)
        on_vector = list(ADD_ON_VECTOR)

        def qk_epilogue(acc, pr, cb, m):
            t = m % 2
            ss = work.tile([P, 4], F32, tag="ss", bufs=8, name="ss")
            for h in range(4):
                junk = work.tile([P, DH], F32, tag="junk", bufs=4, name="junk")
                nc.scalar.activation(
                    out=junk[:], in_=acc[:, DH * h : DH * (h + 1)], func=ACT.Square, accum_out=ss[:, h : h + 1]
                )
            rinv = work.tile([P, 4], F32, tag="rinv", bufs=8, name="rinv")
            nc.scalar.activation(
                out=rinv[:], in_=ss[:], func=ACT.Abs_reciprocal_sqrt, scale=1.0 / (DH * D_IN), bias=EPS / D_IN
            )
            if (t, cb) not in built:
                build_tables(t, cb)
            if not pair:
                prod_new = work.tile([P, 8, 2, DH], F32, tag="prod", bufs=9, name="prod", align_bytes=256)
                pair.append(prod_new)
            prod = pair[0]
            base = 4 * (len(pair) - 1)
            pair.append((pr, cb, m))
            for h in range(4):
                nc.vector.scalar_tensor_tensor(
                    out=prod[:, base + h, :, :],
                    in0=acc[:, DH * h : DH * (h + 1)].unsqueeze(1).to_broadcast([P, 2, DH]),
                    scalar=rinv[:, h : h + 1],
                    in1=tab[(t, cb)][:, h, :, :],
                    op0=ALU.mult,
                    op1=ALU.mult,
                )
            if len(pair) == sizes[0] + 1:
                heads = 4 * sizes[0]
                sizes.remove(sizes[0])
                adder = nc.vector if on_vector[0] else nc.gpsimd
                on_vector.remove(on_vector[0])
                adder.tensor_tensor(
                    out=prod[:, 0:heads, 0, :].rearrange("p a (s j) -> p a s j", j=HALF),
                    in0=prod[:, 0:heads, 0, :].rearrange("p a (s j) -> p a s j", j=HALF),
                    in1=prod[:, 0:heads, 1, :].rearrange("p a (s j) -> p a s j", j=HALF)[:, :, ::-1, :],
                    op=ALU.add,
                )
                for i, group in enumerate(pair[1:]):
                    nc.sync.dma_start(out=dest(group[0], group[1], group[2]), in_=prod[:, 4 * i : 4 * i + 4, 0, :])
                pair.clear()

        def v_epilogue(acc, cb, m):
            vo = work.tile([P, 512], F32, tag="vo", bufs=7, name="vo", align_bytes=256)
            nc.scalar.copy(out=vo[:], in_=acc[:])
            nc.scalar.dma_start(out=dest(V, cb, m), in_=vo[:].rearrange("p (h d) -> p h d", d=DH))

        idle_ps = psum.tile([P, 512], F32, tag="acc", name="idle_ps")
        first = []
        for m in M_ORDER:
            acc0 = psum.tile([P, 512], F32, tag="acc", name="acc0")
            first.append(acc0)
        g_ps = []
        for cb in range(2):
            g_half = psum.tile([P, 512], F32, tag="acc", name="g_half%d" % cb)
            g_ps.append(g_half)

        for i in range(N_IDLE_A):
            nc.tensor.matmul(out=idle_ps[:], lhsT=ones[:], rhs=idle_rhs[:], start=True, stop=True)
        for cb in range(2):
            nc.tensor.matmul(out=g_ps[cb][:], lhsT=ones[:], rhs=g_row[:, 512 * cb : 512 * (cb + 1)], start=True, stop=True)
        for i in range(N_IDLE_B):
            nc.tensor.matmul(out=idle_ps[:], lhsT=ones[:], rhs=idle_rhs[:], start=True, stop=True)
        build_tables(0, 0)
        build_tables(1, 0)
        build_tables(0, 1)

        for i, m in enumerate(M_ORDER):
            mx_pass(first[i], Q, 0, m, 0)
        for g in range(1, PASSES):
            for i in range(2):
                mx_pass(first[i], Q, 0, M_ORDER[i], g)
        for i in range(2, 4):
            for g in range(1, PASSES):
                mx_pass(first[i], Q, 0, M_ORDER[i], g)
        for i, m in enumerate(M_ORDER):
            qk_epilogue(first[i], Q, 0, m)

        heavy = [(pr, cb, m) for pr, cb in ((Q, 1), (K, 0), (K, 1)) for m in M_ORDER]
        light = [(V, cb, m) for cb in range(2) for m in M_ORDER]
        rest = []
        for i in range(6):
            rest.extend([heavy[2 * i], heavy[2 * i + 1]])
            if i < V_AMONG:
                rest.append(light[i])
        rest.extend(light[V_AMONG:7])
        for pr, cb, m in rest:
            acc = psum.tile([P, 512], F32, tag="acc", name="acc")
            for g in range(PASSES):
                mx_pass(acc, pr, cb, m, g)
            if pr == V:
                v_epilogue(acc, cb, m)
            else:
                qk_epilogue(acc, pr, cb, m)

        pr, cb, m = light[7]
        for half in range(2):
            acc_h = psum.tile([P, 512], F32, tag="acc", name="acc_h")
            for g in range(PASSES):
                nc.tensor.matmul_mx(
                    out=acc_h[:, 0:256],
                    lhsT=xw[g][:, 256 * m : 256 * (m + 1)].bitcast(FP4),
                    lhsT_scale=xs[:, g, P * m : P * (m + 1)],
                    rhs=wv[:, g, 1024 * cb + 512 * half : 1024 * cb + 512 * (half + 1)].bitcast(FP4),
                    rhs_scale=ws[V][:, g, 512 * cb + 256 * half : 512 * cb + 256 * (half + 1)],
                    start=(g == 0),
                    stop=(g == PASSES - 1),
                )
            vh = work.tile([P, 256], F32, tag="vh", bufs=2, name="vh", align_bytes=256)
            b, t = m // 2, m % 2
            dst = out_v[b, 4 * cb + 2 * half : 4 * cb + 2 * half + 2, P * t : P * (t + 1), :].rearrange("h p d -> p h d")
            nc.scalar.copy(out=vh[:], in_=acc_h[:, 0:256])
            if half == 0:
                nc.scalar.dma_start(out=dst, in_=vh[:].rearrange("p (h d) -> p h d", d=DH))
            else:
                nc.sync.dma_start(out=dst, in_=vh[:].rearrange("p (h d) -> p h d", d=DH))
